import numpy as np
import ml_dtypes


BF16 = ml_dtypes.bfloat16


def bf(x):
    return np.asarray(x, np.float32).astype(BF16)


def f64(x):
    return np.asarray(x).astype(np.float64)


E2M1 = np.array([0.0, 0.5, 1.0, 1.5, 2.0, 3.0, 4.0, 6.0, -0.0, -0.5, -1.0, -1.5, -2.0, -3.0, -4.0, -6.0])


def pack_weight(w, fmt):
    k, n = w.shape
    w = f64(bf(w)).reshape(k // 32, 32, n)
    amax = np.abs(w).max(1)
    if fmt == "e4m3":
        byte = np.frexp(amax)[1] - 1 + 127 - 7
    else:
        mant, ex = np.frexp(amax / 6.0)
        byte = np.where(mant > 0.5, ex, ex - 1) + 127
    byte = np.clip(np.where(amax > 0, byte, 1), 1, 254)
    scaled = (w * np.exp2(127.0 - byte)[:, None, :]).reshape(k, n).astype(np.float32)
    by_word = np.ascontiguousarray(scaled.reshape(k // 512, 128, 4, n).transpose(0, 1, 3, 2))
    if fmt == "e4m3":
        words = by_word.astype(ml_dtypes.float8_e4m3fn).view(np.uint8)
    else:
        c = by_word.astype(ml_dtypes.float4_e2m1fn).view(np.uint8) & 0xF
        words = c[..., 0::2] | (c[..., 1::2] << 4)
    return np.ascontiguousarray(words), np.ascontiguousarray(byte.astype(np.uint8).reshape(k // 512, 16, n))


def unpack_weight(words, scales, fmt):
    g, p, n, _ = words.shape
    if fmt == "e4m3":
        vals = np.ascontiguousarray(words).view(ml_dtypes.float8_e4m3fn).astype(np.float64)
    else:
        nib = np.empty((g, p, n, 4), np.uint8)
        nib[..., 0::2] = words & 0xF
        nib[..., 1::2] = words >> 4
        vals = E2M1[nib]
    vals = vals * np.repeat(np.exp2(scales.astype(np.float64) - 127.0), 8, axis=1)[..., None]
    return vals.transpose(0, 1, 3, 2).reshape(g * 512, n)

def pack4(w):
    words, scales = pack_weight(w, "e2m1")
    return words.reshape(words.shape[0], 128, -1), scales


def unpack4(words, scales):
    return unpack_weight(words.reshape(words.shape[0], 128, -1, 2), scales, "e2m1")


def kspread(k):
    return np.exp2(np.repeat(np.random.randint(-6, 7, k // 32), 32).astype(np.float64))


B, T, E, H, KV, BLK = 1, 256, 4096, 16, 1, 32
HD = E // H
ROPE_BASE = 10000.0


def rotate_half(t):
    d = t.shape[-1] // 2
    return np.concatenate([-t[..., d:], t[..., :d]], axis=-1)


def rope_tables():
    pos = ROPE_BASE ** ((-2.0 * np.arange(0, HD, 2) - 1.0) / HD)
    angles = np.arange(T)[:, None] * pos[None, :]
    rot = np.concatenate([angles, angles], axis=-1)
    return np.cos(rot), np.sin(rot)


def setup_inputs():
    s = kspread(E)
    x = np.random.standard_normal((B, T, E)) * s
    x_words, x_scales = pack4(np.ascontiguousarray(x.reshape(B * T, E).T))
    words, scales = pack4(np.random.standard_normal((E, (H + 2 * KV) * HD)) * 1.25 * E ** -0.5 / s[:, None])
    return {"x_words": x_words, "x_scales": x_scales, "w_attn_words": words, "w_attn_scales": scales}


def reference(x_words, x_scales, w_attn_words, w_attn_scales):
    qkv = unpack4(x_words, x_scales).T.reshape(B, T, E) @ unpack4(w_attn_words, w_attn_scales)
    q = qkv[..., : H * HD].reshape(B, T, H, HD).transpose(0, 2, 1, 3)
    k = qkv[..., H * HD : (H + KV) * HD].reshape(B, T, KV, HD).transpose(0, 2, 1, 3)
    v = qkv[..., (H + KV) * HD :].reshape(B, T, KV, HD).transpose(0, 2, 1, 3)
    cos, sin = rope_tables()
    q = q * cos + rotate_half(q) * sin
    k = k * cos + rotate_half(k) * sin
    return q, k, v

@@ -1,0 +1,180 @@
+import math
+from contextlib import ExitStack
+
+import concourse.mybir as mybir
+
+TOKENS, K, COLS = 256, 4096, 4608
+HEADS, HEAD_DIM = 16, 256
+HALF = HEAD_DIM // 2
+ROPE_BASE = 10000.0
+
+P = 128
+PASSES = K // 512
+BLOCK = 512
+
+FLOPS = 2 * TOKENS * K * COLS
+
+F32 = mybir.dt.float32
+BF16 = mybir.dt.bfloat16
+I32 = mybir.dt.int32
+U8 = mybir.dt.uint8
+FP4X4 = mybir.dt.float4_e2m1fn_x4
+MULT = mybir.AluOpType.mult
+ADD = mybir.AluOpType.add
+SUB = mybir.AluOpType.subtract
+ACT = mybir.ActivationFunctionType
+
+WARM = 8
+
+
+def tile_multiqueryattention_pa_kernel(tc, x_words, x_scales, w_words, w_scales, q_rot, k_rot, v_out):
+    nc = tc.nc
+    with ExitStack() as ctx:
+        keep = ctx.enter_context(tc.tile_pool(name="keep", bufs=1))
+        work = ctx.enter_context(tc.tile_pool(name="work", bufs=3))
+        outs = ctx.enter_context(tc.tile_pool(name="outs", bufs=22))
+        psum = ctx.enter_context(tc.psum_pool(name="psum", bufs=8))
+        ctx.enter_context(tc.manual_schedule())
+
+        groups = [(0, 512), (512, 1536), (1536, 2560), (2560, 3584), (3584, 4608)]
+        xc = keep.tile([P, PASSES, 2 * TOKENS], U8, name="xc", align_bytes=64)
+        xs = keep.tile([P, PASSES, TOKENS], U8, name="xs", align_bytes=64)
+        wc = []
+        ws = []
+        for i, (lo, hi) in enumerate(groups):
+            wc_i = keep.tile([P, PASSES, 2 * (hi - lo)], U8, name="wc%d" % i, align_bytes=64)
+            ws_i = keep.tile([P, PASSES, hi - lo], U8, name="ws%d" % i, align_bytes=64)
+            wc.append(wc_i)
+            ws.append(ws_i)
+        ones = keep.tile([P, BLOCK], BF16, name="ones", align_bytes=64)
+        pos = keep.tile([P, 2], F32, name="pos")
+        turns = keep.tile([P, 2, 2, HALF], F32, name="turns")
+        whole = keep.tile([P, 2, 2, HALF], I32, name="whole")
+        table = keep.tile([P, 2, 2, HEAD_DIM], F32, name="table")
+        warm_in = keep.tile([P, 1], F32, name="warm_in")
+
+        nc.gpsimd.memset(ones[:], 1.0)
+        nc.vector.memset(xs[:].bitcast(I32), 0)
+        nc.vector.memset(ws[0][:, 0:2, :].bitcast(I32), 0)
+        nc.vector.memset(ws[0][:, 2:8, :].bitcast(I32), 0)
+        nc.gpsimd.iota(pos[:], pattern=[[P, 2]], base=0, channel_multiplier=1, allow_small_or_imprecise_dtypes=True)
+        nc.gpsimd.memset(warm_in[:], 0.0)
+        for i in range(1, 5):
+            nc.gpsimd.memset(ws[i][:].bitcast(I32), 0)
+        nc.scalar.activation(out=warm_in[:], in_=warm_in[:], func=ACT.Sin)
+
+        def load_x(a, b):
+            nc.sync.dma_start(out=xc[:, a:b, :].bitcast(I32), in_=x_words[a:b].rearrange("g p n -> p g n").bitcast(I32))
+
+        def load_w(i, a, b):
+            lo, hi = groups[i]
+            nc.sync.dma_start(out=wc[i][:, a:b, :].bitcast(I32), in_=w_words[a:b, :, 2 * lo : 2 * hi].rearrange("g p n -> p g n").bitcast(I32))
+
+        def load_xs():
+            for quad in range(4):
+                nc.sync.dma_start(out=xs[32 * quad : 32 * quad + 4, :, :].bitcast(I32), in_=x_scales[:, 4 * quad : 4 * quad + 4, :].rearrange("g r n -> r g n").bitcast(I32))
+
+        def load_ws(i, a, b):
+            lo, hi = groups[i]
+            for quad in range(4):
+                nc.sync.dma_start(out=ws[i][32 * quad : 32 * quad + 4, a:b, :].bitcast(I32), in_=w_scales[a:b, 4 * quad : 4 * quad + 4, lo:hi].rearrange("g r n -> r g n").bitcast(I32))
+
+        load_x(0, 2)
+        load_w(0, 0, 1)
+        load_xs()
+        load_ws(0, 0, 2)
+        load_w(0, 1, 2)
+        load_x(2, 8)
+        load_w(0, 2, 4)
+        load_ws(0, 2, 8)
+        load_w(0, 4, 8)
+        for i in range(1, 5):
+            load_ws(i, 0, 8)
+            for a in range(0, 8, 2):
+                load_w(i, a, a + 2)
+
+        step = ROPE_BASE ** (-4.0 / HEAD_DIM)
+        nc.vector.tensor_scalar(out=turns[:, 1, :, 0:1], in0=pos[:].unsqueeze(2), scalar1=ROPE_BASE ** (-1.0 / HEAD_DIM) / (2.0 * math.pi), scalar2=None, op0=MULT)
+        w = 1
+        while w < HALF:
+            nc.vector.tensor_scalar(out=turns[:, 1, :, w : 2 * w], in0=turns[:, 1, :, 0:w], scalar1=step**w, scalar2=None, op0=MULT)
+            w *= 2
+        nc.vector.tensor_scalar(out=turns[:, 0, :, :], in0=turns[:, 1, :, :], scalar1=0.25, scalar2=None, op0=ADD)
+        nc.vector.tensor_copy(out=whole[:], in_=turns[:])
+        nc.vector.tensor_tensor(out=turns[:], in0=turns[:], in1=whole[:], op=SUB)
+        nc.scalar.activation(out=table[:, :, 0, :].rearrange("p n (f j) -> p n f j", f=2), in_=turns[:, 0, :, :].unsqueeze(2).to_broadcast([P, 2, 2, HALF]), func=ACT.Sin, scale=2.0 * math.pi)
+        nc.scalar.activation(out=table[:, :, 1, 0:HALF], in_=turns[:, 1, :, :], func=ACT.Sin, scale=2.0 * math.pi)
+        nc.scalar.activation(out=table[:, :, 1, HALF:HEAD_DIM], in_=turns[:, 1, :, :], func=ACT.Sin, scale=-2.0 * math.pi)
+
+        warm = psum.tile([P, BLOCK], F32, name="bank")
+        for i in range(WARM):
+            nc.tensor.matmul(warm[:], lhsT=ones[:, 0:P], rhs=ones[:], start=True, stop=True)
+
+        def mm(acc, i, col, width, n, g):
+            nc.tensor.matmul_mx(
+                out=acc[:, 0:width],
+                lhsT=xc[:, g, 2 * P * n : 2 * P * (n + 1)].bitcast(FP4X4),
+                lhsT_scale=xs[:, g, P * n : P * (n + 1)],
+                rhs=wc[i][:, g, 2 * col : 2 * (col + width)].bitcast(FP4X4),
+                rhs_scale=ws[i][:, g, col : col + width],
+                start=(g == 0),
+                stop=(g == PASSES - 1),
+            )
+
+        pending = []
+
+        def flush():
+            while pending:
+                prod, heads, dst = pending.pop(0)
+                res = outs.tile([P, 2, HEAD_DIM], F32, name="res")
+                nc.vector.tensor_tensor(
+                    out=res[:, 0:heads, :].rearrange("p h (f j) -> p h f j", f=2),
+                    in0=prod[:, 0, 0:heads, :].rearrange("p h (f j) -> p h f j", f=2),
+                    in1=prod[:, 1, 0:heads, :].rearrange("p h (f j) -> p h f j", f=2)[:, :, ::-1, :],
+                    op=ADD,
+                )
+                nc.sync.dma_start(out=dst, in_=res[:, 0:heads, :])
+
+        def rope(acc, n, heads, dst):
+            prod = work.tile([P, 2, 2, HEAD_DIM], F32, name="prod")
+            nc.vector.tensor_tensor(
+                out=prod[:, :, 0:heads, :],
+                in0=acc[:, 0 : heads * HEAD_DIM].rearrange("p (h d) -> p h d", h=heads).unsqueeze(1).to_broadcast([P, 2, heads, HEAD_DIM]),
+                in1=table[:, n, :, :].unsqueeze(2).to_broadcast([P, 2, heads, HEAD_DIM]),
+                op=MULT,
+            )
+            flush()
+            pending.append((prod, heads, dst))
+
+        def q_dst(block, n):
+            return q_rot[0, 2 * block : 2 * block + 2, P * n : P * (n + 1), :].rearrange("h p d -> p h d")
+
+        for i, blocks in ((0, (0,)), (1, (0, 1)), (2, (0,)), (2, (1,)), (3, (0,)), (3, (1,))):
+            accs = []
+            for b in blocks:
+                for n in range(2):
+                    acc = psum.tile([P, BLOCK], F32, name="bank")
+                    accs.append((acc, b, n))
+            for g in range(PASSES):
+                for acc, b, n in accs:
+                    mm(acc, i, BLOCK * b, BLOCK, n, g)
+            for acc, b, n in accs:
+                rope(acc, n, 2, q_dst(groups[i][0] // BLOCK + b, n))
+        for n in range(2):
+            acc = psum.tile([P, BLOCK], F32, name="bank")
+            for g in range(PASSES):
+                mm(acc, 4, 0, BLOCK, n, g)
+            rope(acc, n, 2, q_dst(7, n))
+        for n in range(2):
+            acc = psum.tile([P, BLOCK], F32, name="bank")
+            for g in range(PASSES):
+                mm(acc, 4, BLOCK, HEAD_DIM, n, g)
+            rope(acc, n, 1, k_rot[0, :, P * n : P * (n + 1), :].rearrange("h p d -> p h d"))
+        flush()
+        for n in range(2):
+            acc = psum.tile([P, BLOCK], F32, name="bank")
+            for g in range(PASSES):
+                mm(acc, 4, BLOCK + HEAD_DIM, HEAD_DIM, n, g)
+            res = outs.tile([P, 2, HEAD_DIM], F32, name="res")
+            nc.scalar.copy(out=res[:, 0, :], in_=acc[:, 0:HEAD_DIM])
+            nc.sync.dma_start(out=v_out[0, 0, P * n : P * (n + 1), :], in_=res[:, 0, :])

@@ -76,13 +76,18 @@ def tile_multiqueryattention_pa_kernel(tc, x_words, x_scales, w_words, w_scales,
 
         def load_ws(i, a, b):
             lo, hi = groups[i]
-            for quad in range(4):
-                nc.sync.dma_start(out=ws[i][32 * quad : 32 * quad + 4, a:b, :].bitcast(I32), in_=w_scales[a:b, 4 * quad : 4 * quad + 4, lo:hi].rearrange("g r n -> r g n").bitcast(I32))
+            if i == 0:
+                for quad in range(4):
+                    nc.sync.dma_start(out=ws[i][32 * quad : 32 * quad + 4, a:b, :].bitcast(I32), in_=w_scales[a:b, 4 * quad : 4 * quad + 4, lo:hi].rearrange("g r n -> r g n").bitcast(I32))
+                return
+            for r in range(4):
+                nc.sync.dma_start(out=ws[i][r:P:32, a:b, :].bitcast(I32), in_=w_scales[a:b, r:16:4, lo:hi].rearrange("g q n -> q g n").bitcast(I32))
 
-        load_x(0, 2)
+        load_x(0, 1)
         load_w(0, 0, 1)
         load_xs()
         load_ws(0, 0, 2)
+        load_x(1, 2)
         load_w(0, 1, 2)
         load_x(2, 8)
         load_w(0, 2, 4)

import math
from contextlib import ExitStack

import concourse.mybir as mybir

TOKENS, K, COLS = 256, 4096, 4608
HEADS, HEAD_DIM = 16, 256
HALF = HEAD_DIM // 2
ROPE_BASE = 10000.0

P = 128
PASSES = K // 512
BLOCK = 512

FLOPS = 2 * TOKENS * K * COLS

F32 = mybir.dt.float32
BF16 = mybir.dt.bfloat16
I32 = mybir.dt.int32
U8 = mybir.dt.uint8
FP4X4 = mybir.dt.float4_e2m1fn_x4
MULT = mybir.AluOpType.mult
ADD = mybir.AluOpType.add
SUB = mybir.AluOpType.subtract
ACT = mybir.ActivationFunctionType

WARM = 8


def tile_multiqueryattention_pa_kernel(tc, x_words, x_scales, w_words, w_scales, q_rot, k_rot, v_out):
    nc = tc.nc
    with ExitStack() as ctx:
        keep = ctx.enter_context(tc.tile_pool(name="keep", bufs=1))
        work = ctx.enter_context(tc.tile_pool(name="work", bufs=3))
        outs = ctx.enter_context(tc.tile_pool(name="outs", bufs=22))
        psum = ctx.enter_context(tc.psum_pool(name="psum", bufs=8))
        ctx.enter_context(tc.manual_schedule())

        groups = [(0, 512), (512, 1536), (1536, 2560), (2560, 3584), (3584, 4608)]
        xc = keep.tile([P, PASSES, 2 * TOKENS], U8, name="xc", align_bytes=64)
        xs = keep.tile([P, PASSES, TOKENS], U8, name="xs", align_bytes=64)
        wc = []
        ws = []
        for i, (lo, hi) in enumerate(groups):
            wc_i = keep.tile([P, PASSES, 2 * (hi - lo)], U8, name="wc%d" % i, align_bytes=64)
            ws_i = keep.tile([P, PASSES, hi - lo], U8, name="ws%d" % i, align_bytes=64)
            wc.append(wc_i)
            ws.append(ws_i)
        ones = keep.tile([P, BLOCK], BF16, name="ones", align_bytes=64)
        pos = keep.tile([P, 2], F32, name="pos")
        turns = keep.tile([P, 2, 2, HALF], F32, name="turns")
        whole = keep.tile([P, 2, 2, HALF], I32, name="whole")
        table = keep.tile([P, 2, 2, HEAD_DIM], F32, name="table")
        warm_in = keep.tile([P, 1], F32, name="warm_in")

        nc.gpsimd.memset(ones[:], 1.0)
        nc.vector.memset(xs[:].bitcast(I32), 0)
        nc.vector.memset(ws[0][:, 0:2, :].bitcast(I32), 0)
        nc.vector.memset(ws[0][:, 2:8, :].bitcast(I32), 0)
        nc.gpsimd.iota(pos[:], pattern=[[P, 2]], base=0, channel_multiplier=1, allow_small_or_imprecise_dtypes=True)
        nc.gpsimd.memset(warm_in[:], 0.0)
        for i in range(1, 5):
            nc.gpsimd.memset(ws[i][:].bitcast(I32), 0)
        nc.scalar.activation(out=warm_in[:], in_=warm_in[:], func=ACT.Sin)

        def load_x(a, b):
            nc.sync.dma_start(out=xc[:, a:b, :].bitcast(I32), in_=x_words[a:b].rearrange("g p n -> p g n").bitcast(I32))

        def load_w(i, a, b):
            lo, hi = groups[i]
            nc.sync.dma_start(out=wc[i][:, a:b, :].bitcast(I32), in_=w_words[a:b, :, 2 * lo : 2 * hi].rearrange("g p n -> p g n").bitcast(I32))

        def load_xs():
            for quad in range(4):
                nc.sync.dma_start(out=xs[32 * quad : 32 * quad + 4, :, :].bitcast(I32), in_=x_scales[:, 4 * quad : 4 * quad + 4, :].rearrange("g r n -> r g n").bitcast(I32))

        def load_ws(i, a, b):
            lo, hi = groups[i]
            if i == 0:
                for quad in range(4):
                    nc.sync.dma_start(out=ws[i][32 * quad : 32 * quad + 4, a:b, :].bitcast(I32), in_=w_scales[a:b, 4 * quad : 4 * quad + 4, lo:hi].rearrange("g r n -> r g n").bitcast(I32))
                return
            for r in range(4):
                nc.sync.dma_start(out=ws[i][r:P:32, a:b, :].bitcast(I32), in_=w_scales[a:b, r:16:4, lo:hi].rearrange("g q n -> q g n").bitcast(I32))

        load_x(0, 1)
        load_w(0, 0, 1)
        load_xs()
        load_ws(0, 0, 2)
        load_x(1, 2)
        load_w(0, 1, 2)
        load_x(2, 8)
        load_w(0, 2, 4)
        load_ws(0, 2, 8)
        load_w(0, 4, 8)
        for i in range(1, 5):
            load_ws(i, 0, 8)
            for a in range(0, 8, 2):
                load_w(i, a, a + 2)

        step = ROPE_BASE ** (-4.0 / HEAD_DIM)
        nc.vector.tensor_scalar(out=turns[:, 1, :, 0:1], in0=pos[:].unsqueeze(2), scalar1=ROPE_BASE ** (-1.0 / HEAD_DIM) / (2.0 * math.pi), scalar2=None, op0=MULT)
        w = 1
        while w < HALF:
            nc.vector.tensor_scalar(out=turns[:, 1, :, w : 2 * w], in0=turns[:, 1, :, 0:w], scalar1=step**w, scalar2=None, op0=MULT)
            w *= 2
        nc.vector.tensor_scalar(out=turns[:, 0, :, :], in0=turns[:, 1, :, :], scalar1=0.25, scalar2=None, op0=ADD)
        nc.vector.tensor_copy(out=whole[:], in_=turns[:])
        nc.vector.tensor_tensor(out=turns[:], in0=turns[:], in1=whole[:], op=SUB)
        nc.scalar.activation(out=table[:, :, 0, :].rearrange("p n (f j) -> p n f j", f=2), in_=turns[:, 0, :, :].unsqueeze(2).to_broadcast([P, 2, 2, HALF]), func=ACT.Sin, scale=2.0 * math.pi)
        nc.scalar.activation(out=table[:, :, 1, 0:HALF], in_=turns[:, 1, :, :], func=ACT.Sin, scale=2.0 * math.pi)
        nc.scalar.activation(out=table[:, :, 1, HALF:HEAD_DIM], in_=turns[:, 1, :, :], func=ACT.Sin, scale=-2.0 * math.pi)

        warm = psum.tile([P, BLOCK], F32, name="bank")
        for i in range(WARM):
            nc.tensor.matmul(warm[:], lhsT=ones[:, 0:P], rhs=ones[:], start=True, stop=True)

        def mm(acc, i, col, width, n, g):
            nc.tensor.matmul_mx(
                out=acc[:, 0:width],
                lhsT=xc[:, g, 2 * P * n : 2 * P * (n + 1)].bitcast(FP4X4),
                lhsT_scale=xs[:, g, P * n : P * (n + 1)],
                rhs=wc[i][:, g, 2 * col : 2 * (col + width)].bitcast(FP4X4),
                rhs_scale=ws[i][:, g, col : col + width],
                start=(g == 0),
                stop=(g == PASSES - 1),
            )

        pending = []

        def flush():
            while pending:
                prod, heads, dst = pending.pop(0)
                res = outs.tile([P, 2, HEAD_DIM], F32, name="res")
                nc.vector.tensor_tensor(
                    out=res[:, 0:heads, :].rearrange("p h (f j) -> p h f j", f=2),
                    in0=prod[:, 0, 0:heads, :].rearrange("p h (f j) -> p h f j", f=2),
                    in1=prod[:, 1, 0:heads, :].rearrange("p h (f j) -> p h f j", f=2)[:, :, ::-1, :],
                    op=ADD,
                )
                nc.sync.dma_start(out=dst, in_=res[:, 0:heads, :])

        def rope(acc, n, heads, dst):
            prod = work.tile([P, 2, 2, HEAD_DIM], F32, name="prod")
            nc.vector.tensor_tensor(
                out=prod[:, :, 0:heads, :],
                in0=acc[:, 0 : heads * HEAD_DIM].rearrange("p (h d) -> p h d", h=heads).unsqueeze(1).to_broadcast([P, 2, heads, HEAD_DIM]),
                in1=table[:, n, :, :].unsqueeze(2).to_broadcast([P, 2, heads, HEAD_DIM]),
                op=MULT,
            )
            flush()
            pending.append((prod, heads, dst))

        def q_dst(block, n):
            return q_rot[0, 2 * block : 2 * block + 2, P * n : P * (n + 1), :].rearrange("h p d -> p h d")

        for i, blocks in ((0, (0,)), (1, (0, 1)), (2, (0,)), (2, (1,)), (3, (0,)), (3, (1,))):
            accs = []
            for b in blocks:
                for n in range(2):
                    acc = psum.tile([P, BLOCK], F32, name="bank")
                    accs.append((acc, b, n))
            for g in range(PASSES):
                for acc, b, n in accs:
                    mm(acc, i, BLOCK * b, BLOCK, n, g)
            for acc, b, n in accs:
                rope(acc, n, 2, q_dst(groups[i][0] // BLOCK + b, n))
        for n in range(2):
            acc = psum.tile([P, BLOCK], F32, name="bank")
            for g in range(PASSES):
                mm(acc, 4, 0, BLOCK, n, g)
            rope(acc, n, 2, q_dst(7, n))
        for n in range(2):
            acc = psum.tile([P, BLOCK], F32, name="bank")
            for g in range(PASSES):
                mm(acc, 4, BLOCK, HEAD_DIM, n, g)
            rope(acc, n, 1, k_rot[0, :, P * n : P * (n + 1), :].rearrange("h p d -> p h d"))
        flush()
        for n in range(2):
            acc = psum.tile([P, BLOCK], F32, name="bank")
            for g in range(PASSES):
                mm(acc, 4, BLOCK + HEAD_DIM, HEAD_DIM, n, g)
            res = outs.tile([P, 2, HEAD_DIM], F32, name="res")
            nc.scalar.copy(out=res[:, 0, :], in_=acc[:, 0:HEAD_DIM])
            nc.sync.dma_start(out=v_out[0, 0, P * n : P * (n + 1), :], in_=res[:, 0, :])
